import numpy as np
import ml_dtypes


def mxq(x, axis, fmt="e4m3"):
    dtype, down = {"e4m3": (ml_dtypes.float8_e4m3fn, 7), "e5m2": (ml_dtypes.float8_e5m2, 14)}[fmt]
    v = np.moveaxis(np.asarray(x, np.float32).astype(ml_dtypes.bfloat16).astype(np.float64), axis, -1)
    blocks = v.reshape(v.shape[:-1] + (-1, 32))
    amax = np.abs(blocks).max(-1, keepdims=True)
    byte = np.maximum(np.where(amax > 0, np.frexp(amax)[1] - 1 + 127, 0) - down, 1)
    scale = np.exp2(byte - 127.0)
    codes = (blocks / scale).astype(np.float32).astype(dtype).astype(np.float64)
    return np.moveaxis((codes * scale).reshape(v.shape), -1, axis)


WIDE = False


def mx_kscale(k):
    if not WIDE:
        return np.ones(k)
    levels = np.array([10, -10, 5, -5, 0])
    a = np.random.permutation(np.resize(levels, k // 512 * 4)).reshape(k // 512, 4)
    idx = np.arange(k)
    return np.exp2(a[idx // 512, idx % 128 // 32])


BF16 = ml_dtypes.bfloat16


def bf(x):
    return np.asarray(x, np.float32).astype(BF16)


def f64(x):
    return np.asarray(x).astype(np.float64)


B, S, H, HS, D = 128, 8, 8, 64, 8192
M = H * HS
FORGET_BIAS = 1.0


def sigmoid(v):
    return 1.0 / (1.0 + np.exp(-v))


def setup_inputs():
    s, t = mx_kscale(M), mx_kscale(D)
    n = np.random.standard_normal
    return {
        'inputs': bf(n((B, D)) * t),
        'h_state': bf(n((B, S, M)) * s),
        'm_state': bf(n((B, S, M))),
        'mem_att': bf(n((B, S, M)) * 2.0),
        'W_g': bf(n((M, M)) * 0.5 / np.sqrt(M)), 'b_g': bf(n(M) * 0.5),
        'W_wf': bf(n((D, M)) / np.sqrt(D) / t[:, None]),
        'W_wi': bf(n((D, M)) / np.sqrt(D) / t[:, None]),
        'W_wo': bf(n((D, M)) / np.sqrt(D) / t[:, None]),
        'W_uf': bf(n((M, M)) / np.sqrt(M) / s[:, None]), 'b_uf': bf(n(M)),
        'W_ui': bf(n((M, M)) / np.sqrt(M) / s[:, None]), 'b_ui': bf(n(M)),
        'W_uo': bf(n((M, M)) / np.sqrt(M) / s[:, None]), 'b_uo': bf(n(M)),
    }


def reference(inputs, h_state, m_state, mem_att, W_g, b_g, W_wf, W_wi, W_wo, W_uf, b_uf, W_ui, b_ui, W_uo, b_uo):
    m = f64(m_state)
    p = f64(mem_att)
    xq = mxq(f64(inputs), 1, 'e4m3')
    hq = mxq(f64(h_state), 2, 'e4m3')
    memory_proposal = ((mxq(p, 2, 'e4m3') @ mxq(f64(W_g), 0, 'e4m3')) + f64(b_g)) + p
    forget_gate = sigmoid((hq @ mxq(f64(W_uf), 0, 'e4m3')) + f64(b_uf) + (xq @ mxq(f64(W_wf), 0, 'e4m3'))[:, None, :])
    input_gate = sigmoid((hq @ mxq(f64(W_ui), 0, 'e4m3')) + f64(b_ui) + (xq @ mxq(f64(W_wi), 0, 'e4m3'))[:, None, :])
    output_gate = sigmoid((hq @ mxq(f64(W_uo), 0, 'e4m3')) + f64(b_uo) + (xq @ mxq(f64(W_wo), 0, 'e4m3'))[:, None, :])
    new_memories = sigmoid(m * forget_gate + FORGET_BIAS) + memory_proposal * sigmoid(input_gate)
    new_hidden = np.tanh(m) * sigmoid(output_gate)
    return new_memories, new_hidden

@@ -1,0 +1,225 @@
+from contextlib import ExitStack
+
+import concourse.mybir as mybir
+from concourse.masks import make_identity
+
+F32 = mybir.dt.float32
+BF16 = mybir.dt.bfloat16
+U32 = mybir.dt.uint32
+U8 = mybir.dt.uint8
+FP8X4 = mybir.dt.float8_e4m3fn_x4
+ADD = mybir.AluOpType.add
+MULT = mybir.AluOpType.mult
+SIGMOID = mybir.ActivationFunctionType.Sigmoid
+TANH = mybir.ActivationFunctionType.Tanh
+
+P = 128
+PACK = 4
+K_PASS = P * PACK
+SLOTS = 8
+WIDTH = 512
+D_IN = 8192
+X_PASSES = D_IN // K_PASS
+CHUNK_PASSES = 4
+FORGET_BIAS = 1.0
+
+FLOPS = 2 * P * D_IN * WIDTH * 3 + 2 * P * SLOTS * WIDTH * WIDTH * 4
+
+
+def cols(index, width):
+    return slice(index * width, (index + 1) * width)
+
+
+def tile_relationalmemorycorecell_pa_k_kernel(
+    tc,
+    inputs,
+    h_state,
+    m_state,
+    mem_att,
+    W_g,
+    b_g,
+    W_wf,
+    W_wi,
+    W_wo,
+    W_uf,
+    b_uf,
+    W_ui,
+    b_ui,
+    W_uo,
+    b_uo,
+    out_0,
+    out_1,
+):
+    nc = tc.nc
+    with ExitStack() as ctx:
+        keep = ctx.enter_context(tc.tile_pool(name="keep", bufs=1))
+        rows_pool = ctx.enter_context(tc.tile_pool(name="rows", bufs=4))
+        turned_pool = ctx.enter_context(tc.tile_pool(name="turned", bufs=2))
+        raw_pool = ctx.enter_context(tc.tile_pool(name="raw", bufs=5))
+        stream = ctx.enter_context(tc.tile_pool(name="stream", bufs=3))
+        work = ctx.enter_context(tc.tile_pool(name="work", bufs=3))
+        turn_psum = ctx.enter_context(tc.psum_pool(name="turn_psum", bufs=2))
+        x_psum = ctx.enter_context(tc.psum_pool(name="x_psum", bufs=2))
+        slot_psum = ctx.enter_context(tc.psum_pool(name="slot_psum", bufs=4))
+
+        identity = keep.tile([P, P], F32)
+        make_identity(nc, identity[:])
+
+        def quantise_rows(rows, codes, scales):
+            words = rows.bitcast(F32).rearrange("b (g p u) -> b g p u", p=P, u=2)
+            turned = turned_pool.tile([P, CHUNK_PASSES * P * PACK], BF16, align_bytes=64)
+            turned_words = turned[:].bitcast(F32).rearrange("p (g b u) -> p g b u", b=P, u=2)
+            for half in range(CHUNK_PASSES // 2):
+                bank = turn_psum.tile([P, 2, 2, P], F32)
+                for g in range(2):
+                    for u in range(2):
+                        nc.tensor.transpose(bank[:, g, u, :], words[:, 2 * half + g, :, u], identity[:])
+                nc.scalar.copy(
+                    out=turned_words[:, cols(half, 2)],
+                    in_=bank[:].rearrange("p g u b -> p g b u"),
+                )
+            nc.vector.quantize_mx(out=codes.bitcast(FP8X4), scales=scales, in_=turned[:])
+
+        def load_weight_pass(raw_pass, rows):
+            nc.sync.dma_start(out=raw_pass, in_=rows.rearrange("(p j) n -> p j n", j=PACK))
+
+        def quantise_weight_pair(raw, codes, scales):
+            grouped = stream.tile([P, 2, WIDTH, PACK], BF16, align_bytes=64)
+            nc.vector.tensor_copy(
+                out=grouped[:, 0].rearrange("p (q i) j -> p q j i", i=4),
+                in_=raw[:, 0].rearrange("p j (q i) -> p q j i", i=4),
+            )
+            nc.scalar.copy(
+                out=grouped[:, 1].rearrange("p (q i) j -> p q j i", i=4),
+                in_=raw[:, 1].rearrange("p j (q i) -> p q j i", i=4),
+            )
+            nc.vector.quantize_mx(
+                out=codes.bitcast(FP8X4),
+                scales=scales,
+                in_=grouped[:].rearrange("p c n j -> p (c n j)"),
+            )
+
+        x_codes = keep.tile([P, X_PASSES * P], U32, align_bytes=64)
+        x_scales = keep.tile([P, X_PASSES * P], U8, align_bytes=64)
+        for c in range(X_PASSES // CHUNK_PASSES):
+            x_rows = rows_pool.tile([P, CHUNK_PASSES * K_PASS], BF16, tag="rows")
+            nc.sync.dma_start(out=x_rows[:], in_=inputs[:, cols(c, CHUNK_PASSES * K_PASS)])
+            quantise_rows(x_rows[:], x_codes[:, cols(c, CHUNK_PASSES * P)], x_scales[:, cols(c, CHUNK_PASSES * P)])
+
+        att = keep.tile([P, SLOTS * WIDTH], BF16)
+        nc.sync.dma_start(out=att[:], in_=mem_att.rearrange("b s m -> b (s m)"))
+        att_codes = keep.tile([P, SLOTS * P], U32, align_bytes=64)
+        att_scales = keep.tile([P, SLOTS * P], U8, align_bytes=64)
+        for c in range(SLOTS // CHUNK_PASSES):
+            quantise_rows(
+                att[:, cols(c, CHUNK_PASSES * K_PASS)],
+                att_codes[:, cols(c, CHUNK_PASSES * P)],
+                att_scales[:, cols(c, CHUNK_PASSES * P)],
+            )
+
+        square_weights = (W_g, W_ui, W_uf, W_uo)
+        biases = (b_g, b_ui, b_uf, b_uo)
+        sq_codes = keep.tile([P, 4 * WIDTH], U32, align_bytes=64)
+        sq_scales = keep.tile([P, 4 * WIDTH], U8, align_bytes=64)
+        bias_rows = keep.tile([P, 4, WIDTH], BF16)
+
+        def quantise_square_pair(pair):
+            raw = raw_pool.tile([P, 2, PACK, WIDTH], BF16, tag="raw")
+            for c in range(2):
+                load_weight_pass(raw[:, c], square_weights[2 * pair + c])
+            quantise_weight_pair(raw, sq_codes[:, cols(pair, 2 * WIDTH)], sq_scales[:, cols(pair, 2 * WIDTH)])
+
+        quantise_square_pair(0)
+        for place in range(4):
+            nc.sync.dma_start(out=bias_rows[:, place, :], in_=biases[place].partition_broadcast(P))
+
+        def slot_product(lhs_codes, lhs_scales, s, place):
+            product = slot_psum.tile([P, WIDTH], F32)
+            nc.tensor.matmul_mx(
+                out=product[:],
+                lhsT=lhs_codes[:, cols(s, P)].bitcast(FP8X4),
+                lhsT_scale=lhs_scales[:, cols(s, P)],
+                rhs=sq_codes[:, cols(place, WIDTH)].bitcast(FP8X4),
+                rhs_scale=sq_scales[:, cols(place, WIDTH)],
+                start=True,
+                stop=True,
+            )
+            return product
+
+        prop = keep.tile([P, SLOTS * WIDTH], F32)
+        for s in range(SLOTS):
+            nc.vector.tensor_tensor(out=prop[:, cols(s, WIDTH)], in0=att[:, cols(s, WIDTH)], in1=bias_rows[:, 0, :], op=ADD)
+            product = slot_product(att_codes, att_scales, s, 0)
+            nc.vector.tensor_tensor(out=prop[:, cols(s, WIDTH)], in0=product[:], in1=prop[:, cols(s, WIDTH)], op=ADD)
+
+        mem = keep.tile([P, SLOTS * WIDTH], BF16)
+        nc.sync.dma_start(out=mem[:], in_=m_state.rearrange("b s m -> b (s m)"))
+        tanh_mem = keep.tile([P, SLOTS * WIDTH], F32)
+        for pair in range(SLOTS // 2):
+            nc.scalar.activation(out=tanh_mem[:, cols(pair, 2 * WIDTH)], in_=mem[:, cols(pair, 2 * WIDTH)], func=TANH)
+
+        h_codes = keep.tile([P, SLOTS * P], U32, align_bytes=64)
+        h_scales = keep.tile([P, SLOTS * P], U8, align_bytes=64)
+        h_flat = h_state.rearrange("b s m -> b (s m)")
+        for c in range(SLOTS // CHUNK_PASSES):
+            h_rows = rows_pool.tile([P, CHUNK_PASSES * K_PASS], BF16, tag="rows")
+            nc.sync.dma_start(out=h_rows[:], in_=h_flat[:, cols(c, CHUNK_PASSES * K_PASS)])
+            quantise_rows(h_rows[:], h_codes[:, cols(c, CHUNK_PASSES * P)], h_scales[:, cols(c, CHUNK_PASSES * P)])
+        quantise_square_pair(1)
+
+        def input_product(weight, place):
+            total = x_psum.tile([P, WIDTH], F32)
+            for pair in range(X_PASSES // 2):
+                raw = raw_pool.tile([P, 2, PACK, WIDTH], BF16, tag="raw")
+                nc.sync.dma_start(
+                    out=raw[:],
+                    in_=weight[cols(pair, 2 * K_PASS), :].rearrange("(c p j) n -> p c j n", p=P, j=PACK),
+                )
+                codes = stream.tile([P, 2 * WIDTH], U32, align_bytes=64)
+                scales = stream.tile([P, 2 * WIDTH], U8, align_bytes=64)
+                quantise_weight_pair(raw, codes[:], scales[:])
+                for c in range(2):
+                    g = 2 * pair + c
+                    nc.tensor.matmul_mx(
+                        out=total[:],
+                        lhsT=x_codes[:, cols(g, P)].bitcast(FP8X4),
+                        lhsT_scale=x_scales[:, cols(g, P)],
+                        rhs=codes[:, cols(c, WIDTH)].bitcast(FP8X4),
+                        rhs_scale=scales[:, cols(c, WIDTH)],
+                        start=(g == 0),
+                        stop=(g == X_PASSES - 1),
+                    )
+            shared = keep.tile([P, WIDTH], F32, name="shared%d" % place)
+            nc.vector.tensor_tensor(out=shared[:], in0=total[:], in1=bias_rows[:, place, :], op=ADD)
+            return shared
+
+        def gate(shared, place, pair):
+            value = work.tile([P, 2 * WIDTH], F32, tag="value")
+            for c in range(2):
+                product = slot_product(h_codes, h_scales, 2 * pair + c, place)
+                nc.vector.tensor_tensor(out=value[:, cols(c, WIDTH)], in0=product[:], in1=shared[:], op=ADD)
+            nc.scalar.activation(out=value[:], in_=value[:], func=SIGMOID)
+            return value
+
+        shared = input_product(W_wi, 1)
+        for pair in range(SLOTS // 2):
+            value = gate(shared, 1, pair)
+            nc.scalar.activation(out=value[:], in_=value[:], func=SIGMOID)
+            nc.vector.tensor_tensor(out=prop[:, cols(pair, 2 * WIDTH)], in0=prop[:, cols(pair, 2 * WIDTH)], in1=value[:], op=MULT)
+
+        shared = input_product(W_wf, 2)
+        for pair in range(SLOTS // 2):
+            value = gate(shared, 2, pair)
+            result = work.tile([P, 2 * WIDTH], F32, tag="result")
+            nc.vector.tensor_tensor(out=result[:], in0=mem[:, cols(pair, 2 * WIDTH)], in1=value[:], op=MULT)
+            nc.scalar.activation(out=result[:], in_=result[:], func=SIGMOID, bias=FORGET_BIAS)
+            nc.vector.tensor_tensor(out=result[:], in0=result[:], in1=prop[:, cols(pair, 2 * WIDTH)], op=ADD)
+            nc.sync.dma_start(out=out_0[:, cols(pair, 2), :], in_=result[:].rearrange("b (s m) -> b s m", s=2))
+
+        shared = input_product(W_wo, 3)
+        for pair in range(SLOTS // 2):
+            value = gate(shared, 3, pair)
+            nc.scalar.activation(out=value[:], in_=value[:], func=SIGMOID)
+            result = work.tile([P, 2 * WIDTH], F32, tag="result")
+            nc.vector.tensor_tensor(out=result[:], in0=tanh_mem[:, cols(pair, 2 * WIDTH)], in1=value[:], op=MULT)
+            nc.sync.dma_start(out=out_1[:, cols(pair, 2), :], in_=result[:].rearrange("b (s m) -> b s m", s=2))

@@ -19,15 +19,41 @@ K_PASS = P * PACK
 SLOTS = 8
 WIDTH = 512
 D_IN = 8192
-X_PASSES = D_IN // K_PASS
-CHUNK_PASSES = 4
 FORGET_BIAS = 1.0
+
+CHUNK_PASSES = 4
+CHUNK = CHUNK_PASSES * K_PASS
+X_CHUNKS = D_IN // CHUNK
+ATT_CHUNKS = SLOTS // CHUNK_PASSES
+CHUNKS = X_CHUNKS + ATT_CHUNKS + ATT_CHUNKS
+X_PASS = 0
+ATT_PASS = X_CHUNKS * CHUNK_PASSES
+H_PASS = ATT_PASS + SLOTS
+
+SQUARE_PAIRS = 2
+GATE_PAIRS = D_IN // (2 * K_PASS)
+PAIRS = SQUARE_PAIRS + 3 * GATE_PAIRS
+RAW_BUFS = 5
+
+PICKUP = 2
+RESIDUAL_FIRST = X_CHUNKS
+PROP_FIRST = X_CHUNKS + 2
+TANH_FIRST = CHUNKS
 
 FLOPS = 2 * P * D_IN * WIDTH * 3 + 2 * P * SLOTS * WIDTH * WIDTH * 4
 
 
 def cols(index, width):
     return slice(index * width, (index + 1) * width)
+
+
+def due(step, first, count=SLOTS):
+    item = step - first
+    return [item] if 0 <= item < count else []
+
+
+def ready(gate):
+    return SQUARE_PAIRS + GATE_PAIRS * (gate + 1)
 
 
 def tile_relationalmemorycorecell_pa_k_kernel(
@@ -51,40 +77,102 @@ def tile_relationalmemorycorecell_pa_k_kernel(
     out_1,
 ):
     nc = tc.nc
+    input_weights = (W_wi, W_wf, W_wo)
+    square_weights = (W_g, W_ui, W_uf, W_uo)
+    biases = (b_g, b_ui, b_uf, b_uo)
+
     with ExitStack() as ctx:
         keep = ctx.enter_context(tc.tile_pool(name="keep", bufs=1))
-        rows_pool = ctx.enter_context(tc.tile_pool(name="rows", bufs=4))
         turned_pool = ctx.enter_context(tc.tile_pool(name="turned", bufs=2))
-        raw_pool = ctx.enter_context(tc.tile_pool(name="raw", bufs=5))
+        raw_pool = ctx.enter_context(tc.tile_pool(name="raw", bufs=RAW_BUFS))
         stream = ctx.enter_context(tc.tile_pool(name="stream", bufs=3))
-        work = ctx.enter_context(tc.tile_pool(name="work", bufs=3))
+        work = ctx.enter_context(tc.tile_pool(name="work", bufs=5))
         turn_psum = ctx.enter_context(tc.psum_pool(name="turn_psum", bufs=2))
         x_psum = ctx.enter_context(tc.psum_pool(name="x_psum", bufs=2))
         slot_psum = ctx.enter_context(tc.psum_pool(name="slot_psum", bufs=4))
+        ctx.enter_context(tc.manual_schedule())
 
         identity = keep.tile([P, P], F32)
         make_identity(nc, identity[:])
 
-        def quantise_rows(rows, codes, scales):
-            words = rows.bitcast(F32).rearrange("b (g p u) -> b g p u", p=P, u=2)
-            turned = turned_pool.tile([P, CHUNK_PASSES * P * PACK], BF16, align_bytes=64)
-            turned_words = turned[:].bitcast(F32).rearrange("p (g b u) -> p g b u", b=P, u=2)
+        rows = keep.tile([P, CHUNKS, CHUNK], BF16)
+        att = rows[:, X_CHUNKS : X_CHUNKS + ATT_CHUNKS, :].rearrange("b c k -> b (c k)")
+        mem = keep.tile([P, SLOTS * WIDTH], BF16)
+        act_codes = keep.tile([P, CHUNKS * CHUNK_PASSES * P], U32, align_bytes=64)
+        act_scales = keep.tile([P, CHUNKS * CHUNK_PASSES * P], U8, align_bytes=64)
+        sq_codes = keep.tile([P, 4 * WIDTH], U32, align_bytes=64)
+        sq_scales = keep.tile([P, 4 * WIDTH], U8, align_bytes=64)
+        bias_rows = keep.tile([P, 4, WIDTH], BF16)
+        prop = keep.tile([P, SLOTS * WIDTH], F32)
+        tanh_mem = keep.tile([P, SLOTS * WIDTH], F32)
+
+        raw_tiles = {}
+        grouped_tiles = {}
+        bank_tiles = {}
+        turned_tiles = {}
+        totals = {}
+        shared = {}
+        products = {}
+        values = {}
+        results = {}
+
+        def load_chunk(c):
+            if c < X_CHUNKS:
+                source = inputs[:, cols(c, CHUNK)]
+            elif c < X_CHUNKS + ATT_CHUNKS:
+                source = mem_att.rearrange("b s m -> b (s m)")[:, cols(c - X_CHUNKS, CHUNK)]
+            else:
+                source = h_state.rearrange("b s m -> b (s m)")[:, cols(c - X_CHUNKS - ATT_CHUNKS, CHUNK)]
+            nc.sync.dma_start(out=rows[:, c, :], in_=source)
+
+        def load_bias(place):
+            nc.sync.dma_start(out=bias_rows[:, place, :], in_=biases[place].partition_broadcast(P))
+
+        def load_pair(t):
+            raw = raw_pool.tile([P, 2, PACK, WIDTH], BF16)
+            raw_tiles[t] = raw
+            if t < SQUARE_PAIRS:
+                for c in range(2):
+                    nc.sync.dma_start(out=raw[:, c], in_=square_weights[2 * t + c].rearrange("(p j) n -> p j n", j=PACK))
+                return
+            gate, pair = divmod(t - SQUARE_PAIRS, GATE_PAIRS)
+            nc.sync.dma_start(
+                out=raw[:],
+                in_=input_weights[gate][cols(pair, 2 * K_PASS), :].rearrange("(c p j) n -> p c j n", p=P, j=PACK),
+            )
+            if pair == GATE_PAIRS - 1:
+                load_bias(gate + 1)
+
+        def transpose_chunk(c):
+            words = rows[:, c, :].bitcast(F32).rearrange("b (g p u) -> b g p u", p=P, u=2)
             for half in range(CHUNK_PASSES // 2):
                 bank = turn_psum.tile([P, 2, 2, P], F32)
+                bank_tiles[(c, half)] = bank
                 for g in range(2):
                     for u in range(2):
                         nc.tensor.transpose(bank[:, g, u, :], words[:, 2 * half + g, :, u], identity[:])
+
+        def collect_chunk(c):
+            turned = turned_pool.tile([P, CHUNK_PASSES * P * PACK], BF16, align_bytes=64)
+            turned_tiles[c] = turned
+            turned_words = turned[:].bitcast(F32).rearrange("p (g b u) -> p g b u", b=P, u=2)
+            for half in range(CHUNK_PASSES // 2):
                 nc.scalar.copy(
                     out=turned_words[:, cols(half, 2)],
-                    in_=bank[:].rearrange("p g u b -> p g b u"),
+                    in_=bank_tiles[(c, half)][:].rearrange("p g u b -> p g b u"),
                 )
-            nc.vector.quantize_mx(out=codes.bitcast(FP8X4), scales=scales, in_=turned[:])
 
-        def load_weight_pass(raw_pass, rows):
-            nc.sync.dma_start(out=raw_pass, in_=rows.rearrange("(p j) n -> p j n", j=PACK))
+        def quantise_chunk(c):
+            nc.vector.quantize_mx(
+                out=act_codes[:, cols(c, CHUNK_PASSES * P)].bitcast(FP8X4),
+                scales=act_scales[:, cols(c, CHUNK_PASSES * P)],
+                in_=turned_tiles[c][:],
+            )
 
-        def quantise_weight_pair(raw, codes, scales):
+        def regroup_pair(t):
+            raw = raw_tiles[t]
             grouped = stream.tile([P, 2, WIDTH, PACK], BF16, align_bytes=64)
+            grouped_tiles[t] = grouped
             nc.vector.tensor_copy(
                 out=grouped[:, 0].rearrange("p (q i) j -> p q j i", i=4),
                 in_=raw[:, 0].rearrange("p j (q i) -> p q j i", i=4),
@@ -93,133 +181,126 @@ def tile_relationalmemorycorecell_pa_k_kernel(
                 out=grouped[:, 1].rearrange("p (q i) j -> p q j i", i=4),
                 in_=raw[:, 1].rearrange("p j (q i) -> p q j i", i=4),
             )
-            nc.vector.quantize_mx(
-                out=codes.bitcast(FP8X4),
-                scales=scales,
-                in_=grouped[:].rearrange("p c n j -> p (c n j)"),
-            )
 
-        x_codes = keep.tile([P, X_PASSES * P], U32, align_bytes=64)
-        x_scales = keep.tile([P, X_PASSES * P], U8, align_bytes=64)
-        for c in range(X_PASSES // CHUNK_PASSES):
-            x_rows = rows_pool.tile([P, CHUNK_PASSES * K_PASS], BF16, tag="rows")
-            nc.sync.dma_start(out=x_rows[:], in_=inputs[:, cols(c, CHUNK_PASSES * K_PASS)])
-            quantise_rows(x_rows[:], x_codes[:, cols(c, CHUNK_PASSES * P)], x_scales[:, cols(c, CHUNK_PASSES * P)])
-
-        att = keep.tile([P, SLOTS * WIDTH], BF16)
-        nc.sync.dma_start(out=att[:], in_=mem_att.rearrange("b s m -> b (s m)"))
-        att_codes = keep.tile([P, SLOTS * P], U32, align_bytes=64)
-        att_scales = keep.tile([P, SLOTS * P], U8, align_bytes=64)
-        for c in range(SLOTS // CHUNK_PASSES):
-            quantise_rows(
-                att[:, cols(c, CHUNK_PASSES * K_PASS)],
-                att_codes[:, cols(c, CHUNK_PASSES * P)],
-                att_scales[:, cols(c, CHUNK_PASSES * P)],
-            )
-
-        square_weights = (W_g, W_ui, W_uf, W_uo)
-        biases = (b_g, b_ui, b_uf, b_uo)
-        sq_codes = keep.tile([P, 4 * WIDTH], U32, align_bytes=64)
-        sq_scales = keep.tile([P, 4 * WIDTH], U8, align_bytes=64)
-        bias_rows = keep.tile([P, 4, WIDTH], BF16)
-
-        def quantise_square_pair(pair):
-            raw = raw_pool.tile([P, 2, PACK, WIDTH], BF16, tag="raw")
+        def quantise_pair(t):
+            grouped = grouped_tiles[t][:].rearrange("p c n j -> p (c n j)")
+            if t < SQUARE_PAIRS:
+                nc.vector.quantize_mx(
+                    out=sq_codes[:, cols(t, 2 * WIDTH)].bitcast(FP8X4),
+                    scales=sq_scales[:, cols(t, 2 * WIDTH)],
+                    in_=grouped,
+                )
+                return
+            codes = stream.tile([P, 2 * WIDTH], U32, align_bytes=64)
+            scales = stream.tile([P, 2 * WIDTH], U8, align_bytes=64)
+            nc.vector.quantize_mx(out=codes[:].bitcast(FP8X4), scales=scales[:], in_=grouped)
+            gate, pair = divmod(t - SQUARE_PAIRS, GATE_PAIRS)
+            if pair == 0:
+                total = x_psum.tile([P, WIDTH], F32)
+                totals[gate] = total
             for c in range(2):
-                load_weight_pass(raw[:, c], square_weights[2 * pair + c])
-            quantise_weight_pair(raw, sq_codes[:, cols(pair, 2 * WIDTH)], sq_scales[:, cols(pair, 2 * WIDTH)])
+                g = 2 * pair + c
+                nc.tensor.matmul_mx(
+                    out=totals[gate][:],
+                    lhsT=act_codes[:, cols(X_PASS + g, P)].bitcast(FP8X4),
+                    lhsT_scale=act_scales[:, cols(X_PASS + g, P)],
+                    rhs=codes[:, cols(c, WIDTH)].bitcast(FP8X4),
+                    rhs_scale=scales[:, cols(c, WIDTH)],
+                    start=(g == 0),
+                    stop=(g == 2 * GATE_PAIRS - 1),
+                )
 
-        quantise_square_pair(0)
-        for place in range(4):
-            nc.sync.dma_start(out=bias_rows[:, place, :], in_=biases[place].partition_broadcast(P))
+        def share(gate):
+            common = keep.tile([P, WIDTH], F32, name="common%d" % gate)
+            shared[gate] = common
+            nc.vector.tensor_tensor(out=common[:], in0=totals[gate][:], in1=bias_rows[:, gate + 1, :], op=ADD)
 
-        def slot_product(lhs_codes, lhs_scales, s, place):
+        def slot_product(first_pass, s, place):
             product = slot_psum.tile([P, WIDTH], F32)
+            products[(place, s)] = product
             nc.tensor.matmul_mx(
                 out=product[:],
-                lhsT=lhs_codes[:, cols(s, P)].bitcast(FP8X4),
-                lhsT_scale=lhs_scales[:, cols(s, P)],
+                lhsT=act_codes[:, cols(first_pass + s, P)].bitcast(FP8X4),
+                lhsT_scale=act_scales[:, cols(first_pass + s, P)],
                 rhs=sq_codes[:, cols(place, WIDTH)].bitcast(FP8X4),
                 rhs_scale=sq_scales[:, cols(place, WIDTH)],
                 start=True,
                 stop=True,
             )
-            return product
 
-        prop = keep.tile([P, SLOTS * WIDTH], F32)
-        for s in range(SLOTS):
-            nc.vector.tensor_tensor(out=prop[:, cols(s, WIDTH)], in0=att[:, cols(s, WIDTH)], in1=bias_rows[:, 0, :], op=ADD)
-            product = slot_product(att_codes, att_scales, s, 0)
-            nc.vector.tensor_tensor(out=prop[:, cols(s, WIDTH)], in0=product[:], in1=prop[:, cols(s, WIDTH)], op=ADD)
+        def gate_sum(gate, s):
+            value = work.tile([P, WIDTH], F32)
+            values[(gate, s)] = value
+            nc.vector.tensor_tensor(out=value[:], in0=products[(gate + 1, s)][:], in1=shared[gate][:], op=ADD)
 
-        mem = keep.tile([P, SLOTS * WIDTH], BF16)
+        def sigmoid(tile_ap, bias=0.0):
+            nc.scalar.activation(out=tile_ap, in_=tile_ap, func=SIGMOID, bias=bias)
+
+        for t in range(RAW_BUFS):
+            load_pair(t)
+            load_chunk(t)
+        load_bias(0)
         nc.sync.dma_start(out=mem[:], in_=m_state.rearrange("b s m -> b (s m)"))
-        tanh_mem = keep.tile([P, SLOTS * WIDTH], F32)
-        for pair in range(SLOTS // 2):
-            nc.scalar.activation(out=tanh_mem[:, cols(pair, 2 * WIDTH)], in_=mem[:, cols(pair, 2 * WIDTH)], func=TANH)
 
-        h_codes = keep.tile([P, SLOTS * P], U32, align_bytes=64)
-        h_scales = keep.tile([P, SLOTS * P], U8, align_bytes=64)
-        h_flat = h_state.rearrange("b s m -> b (s m)")
-        for c in range(SLOTS // CHUNK_PASSES):
-            h_rows = rows_pool.tile([P, CHUNK_PASSES * K_PASS], BF16, tag="rows")
-            nc.sync.dma_start(out=h_rows[:], in_=h_flat[:, cols(c, CHUNK_PASSES * K_PASS)])
-            quantise_rows(h_rows[:], h_codes[:, cols(c, CHUNK_PASSES * P)], h_scales[:, cols(c, CHUNK_PASSES * P)])
-        quantise_square_pair(1)
+        last_step = ready(2) + 1 + PICKUP + SLOTS - 1
+        for t in range(-1, last_step + 1):
+            if t >= 0:
+                for later in due(t + RAW_BUFS, 0, PAIRS):
+                    load_pair(later)
+                for later in due(t + RAW_BUFS, 0, CHUNKS):
+                    load_chunk(later)
 
-        def input_product(weight, place):
-            total = x_psum.tile([P, WIDTH], F32)
-            for pair in range(X_PASSES // 2):
-                raw = raw_pool.tile([P, 2, PACK, WIDTH], BF16, tag="raw")
-                nc.sync.dma_start(
-                    out=raw[:],
-                    in_=weight[cols(pair, 2 * K_PASS), :].rearrange("(c p j) n -> p c j n", p=P, j=PACK),
-                )
-                codes = stream.tile([P, 2 * WIDTH], U32, align_bytes=64)
-                scales = stream.tile([P, 2 * WIDTH], U8, align_bytes=64)
-                quantise_weight_pair(raw, codes[:], scales[:])
-                for c in range(2):
-                    g = 2 * pair + c
-                    nc.tensor.matmul_mx(
-                        out=total[:],
-                        lhsT=x_codes[:, cols(g, P)].bitcast(FP8X4),
-                        lhsT_scale=x_scales[:, cols(g, P)],
-                        rhs=codes[:, cols(c, WIDTH)].bitcast(FP8X4),
-                        rhs_scale=scales[:, cols(c, WIDTH)],
-                        start=(g == 0),
-                        stop=(g == X_PASSES - 1),
-                    )
-            shared = keep.tile([P, WIDTH], F32, name="shared%d" % place)
-            nc.vector.tensor_tensor(out=shared[:], in0=total[:], in1=bias_rows[:, place, :], op=ADD)
-            return shared
+            for s in due(t, PROP_FIRST):
+                slot_product(ATT_PASS, s, 0)
+            for gate in range(3):
+                for s in due(t, ready(gate)):
+                    slot_product(H_PASS, s, gate + 1)
+            for c in due(t, 0, CHUNKS):
+                transpose_chunk(c)
 
-        def gate(shared, place, pair):
-            value = work.tile([P, 2 * WIDTH], F32, tag="value")
-            for c in range(2):
-                product = slot_product(h_codes, h_scales, 2 * pair + c, place)
-                nc.vector.tensor_tensor(out=value[:, cols(c, WIDTH)], in0=product[:], in1=shared[:], op=ADD)
-            nc.scalar.activation(out=value[:], in_=value[:], func=SIGMOID)
-            return value
+            for gate in range(3):
+                for s in due(t, ready(gate) + 1):
+                    gate_sum(gate, s)
+            for s in due(t, RESIDUAL_FIRST):
+                nc.vector.tensor_tensor(out=prop[:, cols(s, WIDTH)], in0=att[:, cols(s, WIDTH)], in1=bias_rows[:, 0, :], op=ADD)
+            for s in due(t, PROP_FIRST + 1):
+                nc.vector.tensor_tensor(out=prop[:, cols(s, WIDTH)], in0=products[(0, s)][:], in1=prop[:, cols(s, WIDTH)], op=ADD)
+            for s in due(t, ready(0) + 1 + PICKUP):
+                nc.vector.tensor_tensor(out=prop[:, cols(s, WIDTH)], in0=prop[:, cols(s, WIDTH)], in1=values[(0, s)][:], op=MULT)
+            for s in due(t, ready(1) + 1 + PICKUP):
+                result = work.tile([P, WIDTH], F32)
+                results[(1, s)] = result
+                nc.vector.tensor_tensor(out=result[:], in0=mem[:, cols(s, WIDTH)], in1=values[(1, s)][:], op=MULT)
+            for s in due(t, ready(1) + 1 + 2 * PICKUP):
+                result = results[(1, s)]
+                nc.vector.tensor_tensor(out=result[:], in0=result[:], in1=prop[:, cols(s, WIDTH)], op=ADD)
+                nc.sync.dma_start(out=out_0[:, s, :], in_=result[:])
+            for s in due(t, ready(2) + 1 + PICKUP):
+                result = work.tile([P, WIDTH], F32)
+                nc.vector.tensor_tensor(out=result[:], in0=tanh_mem[:, cols(s, WIDTH)], in1=values[(2, s)][:], op=MULT)
+                nc.sync.dma_start(out=out_1[:, s, :], in_=result[:])
 
-        shared = input_product(W_wi, 1)
-        for pair in range(SLOTS // 2):
-            value = gate(shared, 1, pair)
-            nc.scalar.activation(out=value[:], in_=value[:], func=SIGMOID)
-            nc.vector.tensor_tensor(out=prop[:, cols(pair, 2 * WIDTH)], in0=prop[:, cols(pair, 2 * WIDTH)], in1=value[:], op=MULT)
+            for later in due(t + 1, 0, PAIRS):
+                regroup_pair(later)
+            for c in due(t, 0, CHUNKS):
+                collect_chunk(c)
+            for c in due(t, 1, CHUNKS):
+                quantise_chunk(c)
+            for gate in range(3):
+                if t == ready(gate):
+                    share(gate)
+            for now in due(t, 0, PAIRS):
+                quantise_pair(now)
 
-        shared = input_product(W_wf, 2)
-        for pair in range(SLOTS // 2):
-            value = gate(shared, 2, pair)
-            result = work.tile([P, 2 * WIDTH], F32, tag="result")
-            nc.vector.tensor_tensor(out=result[:], in0=mem[:, cols(pair, 2 * WIDTH)], in1=value[:], op=MULT)
-            nc.scalar.activation(out=result[:], in_=result[:], func=SIGMOID, bias=FORGET_BIAS)
-            nc.vector.tensor_tensor(out=result[:], in0=result[:], in1=prop[:, cols(pair, 2 * WIDTH)], op=ADD)
-            nc.sync.dma_start(out=out_0[:, cols(pair, 2), :], in_=result[:].rearrange("b (s m) -> b s m", s=2))
-
-        shared = input_product(W_wo, 3)
-        for pair in range(SLOTS // 2):
-            value = gate(shared, 3, pair)
-            nc.scalar.activation(out=value[:], in_=value[:], func=SIGMOID)
-            result = work.tile([P, 2 * WIDTH], F32, tag="result")
-            nc.vector.tensor_tensor(out=result[:], in0=tanh_mem[:, cols(pair, 2 * WIDTH)], in1=value[:], op=MULT)
-            nc.sync.dma_start(out=out_1[:, cols(pair, 2), :], in_=result[:].rearrange("b (s m) -> b s m", s=2))
+            for two in due(t, TANH_FIRST, SLOTS // 2):
+                nc.scalar.activation(out=tanh_mem[:, cols(two, 2 * WIDTH)], in_=mem[:, cols(two, 2 * WIDTH)], func=TANH)
+            for s in due(t, ready(0) + 1):
+                sigmoid(values[(0, s)][:])
+                sigmoid(values[(0, s)][:])
+            for s in due(t, ready(1) + 1):
+                sigmoid(values[(1, s)][:])
+            for s in due(t, ready(1) + 1 + PICKUP):
+                sigmoid(results[(1, s)][:], bias=FORGET_BIAS)
+            for s in due(t, ready(2) + 1):
+                sigmoid(values[(2, s)][:])
+                sigmoid(values[(2, s)][:])

@@ -7,6 +7,7 @@ F32 = mybir.dt.float32
 BF16 = mybir.dt.bfloat16
 U32 = mybir.dt.uint32
 U8 = mybir.dt.uint8
+I32 = mybir.dt.int32
 FP8X4 = mybir.dt.float8_e4m3fn_x4
 ADD = mybir.AluOpType.add
 MULT = mybir.AluOpType.mult
@@ -25,10 +26,10 @@ CHUNK_PASSES = 4
 CHUNK = CHUNK_PASSES * K_PASS
 X_CHUNKS = D_IN // CHUNK
 ATT_CHUNKS = SLOTS // CHUNK_PASSES
-CHUNKS = X_CHUNKS + ATT_CHUNKS + ATT_CHUNKS
-X_PASS = 0
-ATT_PASS = X_CHUNKS * CHUNK_PASSES
-H_PASS = ATT_PASS + SLOTS
+CHUNKS = ATT_CHUNKS + X_CHUNKS + ATT_CHUNKS
+ATT_PASS = 0
+X_PASS = ATT_PASS + SLOTS
+H_PASS = X_PASS + X_CHUNKS * CHUNK_PASSES
 
 SQUARE_PAIRS = 2
 GATE_PAIRS = D_IN // (2 * K_PASS)
@@ -36,9 +37,9 @@ PAIRS = SQUARE_PAIRS + 3 * GATE_PAIRS
 RAW_BUFS = 5
 
 PICKUP = 2
-RESIDUAL_FIRST = X_CHUNKS
-PROP_FIRST = X_CHUNKS + 2
-TANH_FIRST = CHUNKS
+CHUNK_FIRST = -1
+PROP_FIRST = CHUNK_FIRST + 2
+TANH_FIRST = CHUNK_FIRST + CHUNKS
 
 FLOPS = 2 * P * D_IN * WIDTH * 3 + 2 * P * SLOTS * WIDTH * WIDTH * 4
 
@@ -79,7 +80,7 @@ def tile_relationalmemorycorecell_pa_k_kernel(
     nc = tc.nc
     input_weights = (W_wi, W_wf, W_wo)
     square_weights = (W_g, W_ui, W_uf, W_uo)
-    biases = (b_g, b_ui, b_uf, b_uo)
+    gate_biases = (b_ui, b_uf, b_uo)
 
     with ExitStack() as ctx:
         keep = ctx.enter_context(tc.tile_pool(name="keep", bufs=1))
@@ -88,21 +89,32 @@ def tile_relationalmemorycorecell_pa_k_kernel(
         stream = ctx.enter_context(tc.tile_pool(name="stream", bufs=3))
         work = ctx.enter_context(tc.tile_pool(name="work", bufs=5))
         turn_psum = ctx.enter_context(tc.psum_pool(name="turn_psum", bufs=2))
-        x_psum = ctx.enter_context(tc.psum_pool(name="x_psum", bufs=2))
+        x_psum = ctx.enter_context(tc.psum_pool(name="x_psum", bufs=1))
+        bias_psum = ctx.enter_context(tc.psum_pool(name="bias_psum", bufs=1))
         slot_psum = ctx.enter_context(tc.psum_pool(name="slot_psum", bufs=4))
         ctx.enter_context(tc.manual_schedule())
 
+        b_g_row = keep.tile([P, WIDTH], BF16)
+        nc.vector.memset(b_g_row[:].bitcast(I32), 0)
+        nc.sync.dma_start(out=b_g_row[0:1, :], in_=b_g.unsqueeze(0))
+        ones = keep.tile([P, P], BF16)
+        nc.gpsimd.memset(ones[:], 1.0)
         identity = keep.tile([P, P], F32)
         make_identity(nc, identity[:])
+        b_g_rows = bias_psum.tile([P, WIDTH], F32)
+        nc.tensor.matmul(out=b_g_rows[:], lhsT=ones[:], rhs=b_g_row[:], start=True, stop=True)
+
+        warm = keep.tile([P, 1], F32)
+        nc.scalar.activation(out=warm[:], in_=ones[:, 0:1], func=SIGMOID)
 
         rows = keep.tile([P, CHUNKS, CHUNK], BF16)
-        att = rows[:, X_CHUNKS : X_CHUNKS + ATT_CHUNKS, :].rearrange("b c k -> b (c k)")
+        att = rows[:, 0:ATT_CHUNKS, :].rearrange("b c k -> b (c k)")
         mem = keep.tile([P, SLOTS * WIDTH], BF16)
         act_codes = keep.tile([P, CHUNKS * CHUNK_PASSES * P], U32, align_bytes=64)
         act_scales = keep.tile([P, CHUNKS * CHUNK_PASSES * P], U8, align_bytes=64)
         sq_codes = keep.tile([P, 4 * WIDTH], U32, align_bytes=64)
         sq_scales = keep.tile([P, 4 * WIDTH], U8, align_bytes=64)
-        bias_rows = keep.tile([P, 4, WIDTH], BF16)
+        bias_rows = keep.tile([P, 3, WIDTH], BF16)
         prop = keep.tile([P, SLOTS * WIDTH], F32)
         tanh_mem = keep.tile([P, SLOTS * WIDTH], F32)
 
@@ -117,16 +129,16 @@ def tile_relationalmemorycorecell_pa_k_kernel(
         results = {}
 
         def load_chunk(c):
-            if c < X_CHUNKS:
-                source = inputs[:, cols(c, CHUNK)]
-            elif c < X_CHUNKS + ATT_CHUNKS:
-                source = mem_att.rearrange("b s m -> b (s m)")[:, cols(c - X_CHUNKS, CHUNK)]
+            if c < ATT_CHUNKS:
+                source = mem_att.rearrange("b s m -> b (s m)")[:, cols(c, CHUNK)]
+            elif c < ATT_CHUNKS + X_CHUNKS:
+                source = inputs[:, cols(c - ATT_CHUNKS, CHUNK)]
             else:
-                source = h_state.rearrange("b s m -> b (s m)")[:, cols(c - X_CHUNKS - ATT_CHUNKS, CHUNK)]
+                source = h_state.rearrange("b s m -> b (s m)")[:, cols(c - ATT_CHUNKS - X_CHUNKS, CHUNK)]
             nc.sync.dma_start(out=rows[:, c, :], in_=source)
 
-        def load_bias(place):
-            nc.sync.dma_start(out=bias_rows[:, place, :], in_=biases[place].partition_broadcast(P))
+        def load_bias(gate):
+            nc.sync.dma_start(out=bias_rows[:, gate, :], in_=gate_biases[gate].partition_broadcast(P))
 
         def load_pair(t):
             raw = raw_pool.tile([P, 2, PACK, WIDTH], BF16)
@@ -141,7 +153,7 @@ def tile_relationalmemorycorecell_pa_k_kernel(
                 in_=input_weights[gate][cols(pair, 2 * K_PASS), :].rearrange("(c p j) n -> p c j n", p=P, j=PACK),
             )
             if pair == GATE_PAIRS - 1:
-                load_bias(gate + 1)
+                load_bias(gate)
 
         def transpose_chunk(c):
             words = rows[:, c, :].bitcast(F32).rearrange("b (g p u) -> b g p u", p=P, u=2)
@@ -213,7 +225,7 @@ def tile_relationalmemorycorecell_pa_k_kernel(
         def share(gate):
             common = keep.tile([P, WIDTH], F32, name="common%d" % gate)
             shared[gate] = common
-            nc.vector.tensor_tensor(out=common[:], in0=totals[gate][:], in1=bias_rows[:, gate + 1, :], op=ADD)
+            nc.vector.tensor_tensor(out=common[:], in0=totals[gate][:], in1=bias_rows[:, gate, :], op=ADD)
 
         def slot_product(first_pass, s, place):
             product = slot_psum.tile([P, WIDTH], F32)
@@ -239,10 +251,9 @@ def tile_relationalmemorycorecell_pa_k_kernel(
         for t in range(RAW_BUFS):
             load_pair(t)
             load_chunk(t)
-        load_bias(0)
         nc.sync.dma_start(out=mem[:], in_=m_state.rearrange("b s m -> b (s m)"))
 
-        last_step = ready(2) + 1 + PICKUP + SLOTS - 1
+        last_step = ready(2) + 2 + PICKUP + SLOTS - 1
         for t in range(-1, last_step + 1):
             if t >= 0:
                 for later in due(t + RAW_BUFS, 0, PAIRS):
@@ -255,17 +266,17 @@ def tile_relationalmemorycorecell_pa_k_kernel(
             for gate in range(3):
                 for s in due(t, ready(gate)):
                     slot_product(H_PASS, s, gate + 1)
-            for c in due(t, 0, CHUNKS):
+            for c in due(t, CHUNK_FIRST, CHUNKS):
                 transpose_chunk(c)
 
             for gate in range(3):
                 for s in due(t, ready(gate) + 1):
                     gate_sum(gate, s)
-            for s in due(t, RESIDUAL_FIRST):
-                nc.vector.tensor_tensor(out=prop[:, cols(s, WIDTH)], in0=att[:, cols(s, WIDTH)], in1=bias_rows[:, 0, :], op=ADD)
+            for s in due(t, PROP_FIRST - 1):
+                nc.vector.tensor_tensor(out=prop[:, cols(s, WIDTH)], in0=b_g_rows[:], in1=att[:, cols(s, WIDTH)], op=ADD)
             for s in due(t, PROP_FIRST + 1):
                 nc.vector.tensor_tensor(out=prop[:, cols(s, WIDTH)], in0=products[(0, s)][:], in1=prop[:, cols(s, WIDTH)], op=ADD)
-            for s in due(t, ready(0) + 1 + PICKUP):
+            for s in due(t, ready(0) + 2 + PICKUP):
                 nc.vector.tensor_tensor(out=prop[:, cols(s, WIDTH)], in0=prop[:, cols(s, WIDTH)], in1=values[(0, s)][:], op=MULT)
             for s in due(t, ready(1) + 1 + PICKUP):
                 result = work.tile([P, WIDTH], F32)
@@ -275,16 +286,16 @@ def tile_relationalmemorycorecell_pa_k_kernel(
                 result = results[(1, s)]
                 nc.vector.tensor_tensor(out=result[:], in0=result[:], in1=prop[:, cols(s, WIDTH)], op=ADD)
                 nc.sync.dma_start(out=out_0[:, s, :], in_=result[:])
-            for s in due(t, ready(2) + 1 + PICKUP):
+            for s in due(t, ready(2) + 2 + PICKUP):
                 result = work.tile([P, WIDTH], F32)
                 nc.vector.tensor_tensor(out=result[:], in0=tanh_mem[:, cols(s, WIDTH)], in1=values[(2, s)][:], op=MULT)
                 nc.sync.dma_start(out=out_1[:, s, :], in_=result[:])
 
             for later in due(t + 1, 0, PAIRS):
                 regroup_pair(later)
-            for c in due(t, 0, CHUNKS):
+            for c in due(t, CHUNK_FIRST, CHUNKS):
                 collect_chunk(c)
-            for c in due(t, 1, CHUNKS):
+            for c in due(t, CHUNK_FIRST + 1, CHUNKS):
                 quantise_chunk(c)
             for gate in range(3):
                 if t == ready(gate):
@@ -294,13 +305,12 @@ def tile_relationalmemorycorecell_pa_k_kernel(
 
             for two in due(t, TANH_FIRST, SLOTS // 2):
                 nc.scalar.activation(out=tanh_mem[:, cols(two, 2 * WIDTH)], in_=mem[:, cols(two, 2 * WIDTH)], func=TANH)
-            for s in due(t, ready(0) + 1):
-                sigmoid(values[(0, s)][:])
-                sigmoid(values[(0, s)][:])
+            for gate in (0, 2):
+                for s in due(t, ready(gate) + 1):
+                    sigmoid(values[(gate, s)][:])
+                for s in due(t, ready(gate) + 2):
+                    sigmoid(values[(gate, s)][:])
             for s in due(t, ready(1) + 1):
                 sigmoid(values[(1, s)][:])
             for s in due(t, ready(1) + 1 + PICKUP):
                 sigmoid(results[(1, s)][:], bias=FORGET_BIAS)
-            for s in due(t, ready(2) + 1):
-                sigmoid(values[(2, s)][:])
-                sigmoid(values[(2, s)][:])

@@ -36,6 +36,9 @@ GATE_PAIRS = D_IN // (2 * K_PASS)
 PAIRS = SQUARE_PAIRS + 3 * GATE_PAIRS
 RAW_BUFS = 5
 
+TENSOR_FIRST = 11
+TENSOR_COLS = 128
+
 PICKUP = 2
 CHUNK_FIRST = -1
 PROP_FIRST = CHUNK_FIRST + 2
@@ -101,6 +104,8 @@ def tile_relationalmemorycorecell_pa_k_kernel(
         nc.gpsimd.memset(ones[:], 1.0)
         identity = keep.tile([P, P], F32)
         make_identity(nc, identity[:])
+        identity_b = keep.tile([P, P], BF16)
+        make_identity(nc, identity_b[:])
         b_g_rows = bias_psum.tile([P, WIDTH], F32)
         nc.tensor.matmul(out=b_g_rows[:], lhsT=ones[:], rhs=b_g_row[:], start=True, stop=True)
 
@@ -185,14 +190,28 @@ def tile_relationalmemorycorecell_pa_k_kernel(
             raw = raw_tiles[t]
             grouped = stream.tile([P, 2, WIDTH, PACK], BF16, align_bytes=64)
             grouped_tiles[t] = grouped
+            own = WIDTH
+            if t >= TENSOR_FIRST:
+                own = WIDTH - TENSOR_COLS
+                bank = turn_psum.tile([P, 2, TENSOR_COLS * PACK], BF16)
+                for c in range(2):
+                    nc.tensor.matmul(
+                        out=bank[:, c, :],
+                        lhsT=identity_b[:],
+                        rhs=raw[:, c, :, own:WIDTH].rearrange("p j n -> p n j"),
+                        start=True,
+                        stop=True,
+                    )
             nc.vector.tensor_copy(
-                out=grouped[:, 0].rearrange("p (q i) j -> p q j i", i=4),
-                in_=raw[:, 0].rearrange("p j (q i) -> p q j i", i=4),
+                out=grouped[:, 0, 0:own].rearrange("p (q i) j -> p q j i", i=4),
+                in_=raw[:, 0, :, 0:own].rearrange("p j (q i) -> p q j i", i=4),
             )
             nc.scalar.copy(
-                out=grouped[:, 1].rearrange("p (q i) j -> p q j i", i=4),
-                in_=raw[:, 1].rearrange("p j (q i) -> p q j i", i=4),
+                out=grouped[:, 1, 0:own].rearrange("p (q i) j -> p q j i", i=4),
+                in_=raw[:, 1, :, 0:own].rearrange("p j (q i) -> p q j i", i=4),
             )
+            if t >= TENSOR_FIRST:
+                nc.scalar.copy(out=grouped[:, :, own:WIDTH].rearrange("p c n j -> p c (n j)"), in_=bank[:])
 
         def quantise_pair(t):
             grouped = grouped_tiles[t][:].rearrange("p c n j -> p (c n j)")

@@ -37,7 +37,8 @@ PAIRS = SQUARE_PAIRS + 3 * GATE_PAIRS
 RAW_BUFS = 5
 
 TENSOR_FIRST = 11
-TENSOR_COLS = 128
+TENSOR_COLS = 256
+TENSOR_SPLIT = 128
 
 PICKUP = 2
 CHUNK_FIRST = -1
@@ -193,25 +194,25 @@ def tile_relationalmemorycorecell_pa_k_kernel(
             own = WIDTH
             if t >= TENSOR_FIRST:
                 own = WIDTH - TENSOR_COLS
-                bank = turn_psum.tile([P, 2, TENSOR_COLS * PACK], BF16)
-                for c in range(2):
+                bank = turn_psum.tile([P, TENSOR_COLS, PACK], BF16)
+                for first in range(0, TENSOR_COLS, TENSOR_SPLIT):
                     nc.tensor.matmul(
-                        out=bank[:, c, :],
+                        out=bank[:, first : first + TENSOR_SPLIT, :],
                         lhsT=identity_b[:],
-                        rhs=raw[:, c, :, own:WIDTH].rearrange("p j n -> p n j"),
+                        rhs=raw[:, 1, :, own + first : own + first + TENSOR_SPLIT].rearrange("p j n -> p n j"),
                         start=True,
                         stop=True,
                     )
             nc.vector.tensor_copy(
-                out=grouped[:, 0, 0:own].rearrange("p (q i) j -> p q j i", i=4),
-                in_=raw[:, 0, :, 0:own].rearrange("p j (q i) -> p q j i", i=4),
+                out=grouped[:, 0].rearrange("p (q i) j -> p q j i", i=4),
+                in_=raw[:, 0].rearrange("p j (q i) -> p q j i", i=4),
             )
             nc.scalar.copy(
                 out=grouped[:, 1, 0:own].rearrange("p (q i) j -> p q j i", i=4),
                 in_=raw[:, 1, :, 0:own].rearrange("p j (q i) -> p q j i", i=4),
             )
             if t >= TENSOR_FIRST:
-                nc.scalar.copy(out=grouped[:, :, own:WIDTH].rearrange("p c n j -> p c (n j)"), in_=bank[:])
+                nc.scalar.copy(out=grouped[:, 1, own:WIDTH], in_=bank[:])
 
         def quantise_pair(t):
             grouped = grouped_tiles[t][:].rearrange("p c n j -> p (c n j)")

@@ -38,7 +38,7 @@ RAW_BUFS = 5
 
 TENSOR_FIRST = 11
 TENSOR_COLS = 256
-TENSOR_SPLIT = 128
+VECTOR_COLS = 432
 
 PICKUP = 2
 CHUNK_FIRST = -1
@@ -125,6 +125,7 @@ def tile_relationalmemorycorecell_pa_k_kernel(
         tanh_mem = keep.tile([P, SLOTS * WIDTH], F32)
 
         raw_tiles = {}
+        regroup_banks = {}
         grouped_tiles = {}
         bank_tiles = {}
         turned_tiles = {}
@@ -191,28 +192,36 @@ def tile_relationalmemorycorecell_pa_k_kernel(
             raw = raw_tiles[t]
             grouped = stream.tile([P, 2, WIDTH, PACK], BF16, align_bytes=64)
             grouped_tiles[t] = grouped
-            own = WIDTH
+            vector_cols, scalar_first = WIDTH, 0
             if t >= TENSOR_FIRST:
-                own = WIDTH - TENSOR_COLS
-                bank = turn_psum.tile([P, TENSOR_COLS, PACK], BF16)
-                for first in range(0, TENSOR_COLS, TENSOR_SPLIT):
-                    nc.tensor.matmul(
-                        out=bank[:, first : first + TENSOR_SPLIT, :],
-                        lhsT=identity_b[:],
-                        rhs=raw[:, 1, :, own + first : own + first + TENSOR_SPLIT].rearrange("p j n -> p n j"),
-                        start=True,
-                        stop=True,
-                    )
+                vector_cols, scalar_first = VECTOR_COLS, VECTOR_COLS + TENSOR_COLS - WIDTH
             nc.vector.tensor_copy(
-                out=grouped[:, 0].rearrange("p (q i) j -> p q j i", i=4),
-                in_=raw[:, 0].rearrange("p j (q i) -> p q j i", i=4),
+                out=grouped[:, 0, 0:vector_cols].rearrange("p (q i) j -> p q j i", i=4),
+                in_=raw[:, 0, :, 0:vector_cols].rearrange("p j (q i) -> p q j i", i=4),
             )
             nc.scalar.copy(
-                out=grouped[:, 1, 0:own].rearrange("p (q i) j -> p q j i", i=4),
-                in_=raw[:, 1, :, 0:own].rearrange("p j (q i) -> p q j i", i=4),
+                out=grouped[:, 1, scalar_first:WIDTH].rearrange("p (q i) j -> p q j i", i=4),
+                in_=raw[:, 1, :, scalar_first:WIDTH].rearrange("p j (q i) -> p q j i", i=4),
             )
             if t >= TENSOR_FIRST:
-                nc.scalar.copy(out=grouped[:, 1, own:WIDTH], in_=bank[:])
+                flat = grouped[:].rearrange("p c n j -> p (c n) j")
+                nc.scalar.copy(out=flat[:, VECTOR_COLS : VECTOR_COLS + TENSOR_COLS, :], in_=regroup_banks[t][:])
+
+        def tensor_regroup(t):
+            raw = raw_tiles[t]
+            bank = turn_psum.tile([P, TENSOR_COLS, PACK], BF16)
+            regroup_banks[t] = bank
+            rest = VECTOR_COLS + TENSOR_COLS - WIDTH
+            first = 0
+            for c, begin, end in ((0, VECTOR_COLS, WIDTH), (1, 0, rest // 2), (1, rest // 2, rest)):
+                nc.tensor.matmul(
+                    out=bank[:, first : first + end - begin, :],
+                    lhsT=identity_b[:],
+                    rhs=raw[:, c, :, begin:end].rearrange("p j n -> p n j"),
+                    start=True,
+                    stop=True,
+                )
+                first += end - begin
 
         def quantise_pair(t):
             grouped = grouped_tiles[t][:].rearrange("p c n j -> p (c n j)")
@@ -288,6 +297,9 @@ def tile_relationalmemorycorecell_pa_k_kernel(
                     slot_product(H_PASS, s, gate + 1)
             for c in due(t, CHUNK_FIRST, CHUNKS):
                 transpose_chunk(c)
+            for later in due(t + 2, 0, PAIRS):
+                if later >= TENSOR_FIRST:
+                    tensor_regroup(later)
 
             for gate in range(3):
                 for s in due(t, ready(gate) + 1):

@@ -24,12 +24,8 @@ FORGET_BIAS = 1.0
 
 CHUNK_PASSES = 4
 CHUNK = CHUNK_PASSES * K_PASS
-X_CHUNKS = D_IN // CHUNK
-ATT_CHUNKS = SLOTS // CHUNK_PASSES
-CHUNKS = ATT_CHUNKS + X_CHUNKS + ATT_CHUNKS
-ATT_PASS = 0
-X_PASS = ATT_PASS + SLOTS
-H_PASS = X_PASS + X_CHUNKS * CHUNK_PASSES
+CHUNK_ORDER = ("att0", "x0", "x1", "att1", "x2", "x3", "h0", "h1")
+CHUNKS = len(CHUNK_ORDER)
 
 SQUARE_PAIRS = 2
 GATE_PAIRS = D_IN // (2 * K_PASS)
@@ -38,10 +34,11 @@ RAW_BUFS = 5
 
 TENSOR_FIRST = 11
 TENSOR_COLS = 256
-VECTOR_COLS = 432
+VECTOR_COLS = 384
 
 PICKUP = 2
-CHUNK_FIRST = -1
+CHUNK_FIRST = 0
+CHUNK_AHEAD = 4
 PROP_FIRST = CHUNK_FIRST + 2
 TANH_FIRST = CHUNK_FIRST + CHUNKS
 
@@ -55,6 +52,11 @@ def cols(index, width):
 def due(step, first, count=SLOTS):
     item = step - first
     return [item] if 0 <= item < count else []
+
+
+def act_pass(name, g):
+    chunk, within = divmod(g, CHUNK_PASSES)
+    return CHUNK_ORDER.index(name + "%d" % chunk) * CHUNK_PASSES + within
 
 
 def ready(gate):
@@ -100,13 +102,13 @@ def tile_relationalmemorycorecell_pa_k_kernel(
 
         b_g_row = keep.tile([P, WIDTH], BF16)
         nc.vector.memset(b_g_row[:].bitcast(I32), 0)
-        nc.sync.dma_start(out=b_g_row[0:1, :], in_=b_g.unsqueeze(0))
         ones = keep.tile([P, P], BF16)
         nc.gpsimd.memset(ones[:], 1.0)
         identity = keep.tile([P, P], F32)
         make_identity(nc, identity[:])
         identity_b = keep.tile([P, P], BF16)
         make_identity(nc, identity_b[:])
+        nc.scalar.dma_start(out=b_g_row[0:1, :], in_=b_g.unsqueeze(0))
         b_g_rows = bias_psum.tile([P, WIDTH], F32)
         nc.tensor.matmul(out=b_g_rows[:], lhsT=ones[:], rhs=b_g_row[:], start=True, stop=True)
 
@@ -114,7 +116,7 @@ def tile_relationalmemorycorecell_pa_k_kernel(
         nc.scalar.activation(out=warm[:], in_=ones[:, 0:1], func=SIGMOID)
 
         rows = keep.tile([P, CHUNKS, CHUNK], BF16)
-        att = rows[:, 0:ATT_CHUNKS, :].rearrange("b c k -> b (c k)")
+        slot_rows = rows[:].rearrange("b c (g k) -> b (c g) k", g=CHUNK_PASSES)
         mem = keep.tile([P, SLOTS * WIDTH], BF16)
         act_codes = keep.tile([P, CHUNKS * CHUNK_PASSES * P], U32, align_bytes=64)
         act_scales = keep.tile([P, CHUNKS * CHUNK_PASSES * P], U8, align_bytes=64)
@@ -136,12 +138,13 @@ def tile_relationalmemorycorecell_pa_k_kernel(
         results = {}
 
         def load_chunk(c):
-            if c < ATT_CHUNKS:
-                source = mem_att.rearrange("b s m -> b (s m)")[:, cols(c, CHUNK)]
-            elif c < ATT_CHUNKS + X_CHUNKS:
-                source = inputs[:, cols(c - ATT_CHUNKS, CHUNK)]
-            else:
-                source = h_state.rearrange("b s m -> b (s m)")[:, cols(c - ATT_CHUNKS - X_CHUNKS, CHUNK)]
+            sources = {
+                "x": inputs,
+                "h": h_state.rearrange("b s m -> b (s m)"),
+                "att": mem_att.rearrange("b s m -> b (s m)"),
+            }
+            name = CHUNK_ORDER[c]
+            source = sources[name[:-1]][:, cols(int(name[-1]), CHUNK)]
             nc.sync.dma_start(out=rows[:, c, :], in_=source)
 
         def load_bias(gate):
@@ -150,6 +153,14 @@ def tile_relationalmemorycorecell_pa_k_kernel(
         def load_pair(t):
             raw = raw_pool.tile([P, 2, PACK, WIDTH], BF16)
             raw_tiles[t] = raw
+            if t == 0:
+                for piece in range(2):
+                    for c in range(2):
+                        nc.sync.dma_start(
+                            out=raw[:, c, :, cols(piece, WIDTH // 2)],
+                            in_=square_weights[c].rearrange("(p j) n -> p j n", j=PACK)[:, :, cols(piece, WIDTH // 2)],
+                        )
+                return
             if t < SQUARE_PAIRS:
                 for c in range(2):
                     nc.sync.dma_start(out=raw[:, c], in_=square_weights[2 * t + c].rearrange("(p j) n -> p j n", j=PACK))
@@ -192,17 +203,22 @@ def tile_relationalmemorycorecell_pa_k_kernel(
             raw = raw_tiles[t]
             grouped = stream.tile([P, 2, WIDTH, PACK], BF16, align_bytes=64)
             grouped_tiles[t] = grouped
-            vector_cols, scalar_first = WIDTH, 0
-            if t >= TENSOR_FIRST:
-                vector_cols, scalar_first = VECTOR_COLS, VECTOR_COLS + TENSOR_COLS - WIDTH
-            nc.vector.tensor_copy(
-                out=grouped[:, 0, 0:vector_cols].rearrange("p (q i) j -> p q j i", i=4),
-                in_=raw[:, 0, :, 0:vector_cols].rearrange("p j (q i) -> p q j i", i=4),
-            )
-            nc.scalar.copy(
-                out=grouped[:, 1, scalar_first:WIDTH].rearrange("p (q i) j -> p q j i", i=4),
-                in_=raw[:, 1, :, scalar_first:WIDTH].rearrange("p j (q i) -> p q j i", i=4),
-            )
+            vector_boxes, scalar_boxes = [(0, cols(0, WIDTH))], [(1, cols(0, WIDTH))]
+            if t == 0:
+                vector_boxes = [(0, cols(0, WIDTH // 2)), (0, cols(1, WIDTH // 2)), (1, cols(1, WIDTH // 2))]
+                scalar_boxes = [(1, cols(0, WIDTH // 2))]
+            elif t == 1:
+                vector_boxes = [(0, cols(0, WIDTH)), (1, cols(0, WIDTH // 2))]
+                scalar_boxes = [(1, cols(1, WIDTH // 2))]
+            elif t >= TENSOR_FIRST:
+                vector_boxes = [(0, slice(0, VECTOR_COLS))]
+                scalar_boxes = [(1, slice(VECTOR_COLS + TENSOR_COLS - WIDTH, WIDTH))]
+            for copy, parts in ((nc.vector.tensor_copy, vector_boxes), (nc.scalar.copy, scalar_boxes)):
+                for c, part in parts:
+                    copy(
+                        out=grouped[:, c, part].rearrange("p (q i) j -> p q j i", i=4),
+                        in_=raw[:, c, :, part].rearrange("p j (q i) -> p q j i", i=4),
+                    )
             if t >= TENSOR_FIRST:
                 flat = grouped[:].rearrange("p c n j -> p (c n) j")
                 nc.scalar.copy(out=flat[:, VECTOR_COLS : VECTOR_COLS + TENSOR_COLS, :], in_=regroup_banks[t][:])
@@ -213,7 +229,7 @@ def tile_relationalmemorycorecell_pa_k_kernel(
             regroup_banks[t] = bank
             rest = VECTOR_COLS + TENSOR_COLS - WIDTH
             first = 0
-            for c, begin, end in ((0, VECTOR_COLS, WIDTH), (1, 0, rest // 2), (1, rest // 2, rest)):
+            for c, begin, end in ((0, VECTOR_COLS, WIDTH), (1, 0, rest)):
                 nc.tensor.matmul(
                     out=bank[:, first : first + end - begin, :],
                     lhsT=identity_b[:],
@@ -243,8 +259,8 @@ def tile_relationalmemorycorecell_pa_k_kernel(
                 g = 2 * pair + c
                 nc.tensor.matmul_mx(
                     out=totals[gate][:],
-                    lhsT=act_codes[:, cols(X_PASS + g, P)].bitcast(FP8X4),
-                    lhsT_scale=act_scales[:, cols(X_PASS + g, P)],
+                    lhsT=act_codes[:, cols(act_pass("x", g), P)].bitcast(FP8X4),
+                    lhsT_scale=act_scales[:, cols(act_pass("x", g), P)],
                     rhs=codes[:, cols(c, WIDTH)].bitcast(FP8X4),
                     rhs_scale=scales[:, cols(c, WIDTH)],
                     start=(g == 0),
@@ -256,13 +272,13 @@ def tile_relationalmemorycorecell_pa_k_kernel(
             shared[gate] = common
             nc.vector.tensor_tensor(out=common[:], in0=totals[gate][:], in1=bias_rows[:, gate, :], op=ADD)
 
-        def slot_product(first_pass, s, place):
+        def slot_product(name, s, place):
             product = slot_psum.tile([P, WIDTH], F32)
             products[(place, s)] = product
             nc.tensor.matmul_mx(
                 out=product[:],
-                lhsT=act_codes[:, cols(first_pass + s, P)].bitcast(FP8X4),
-                lhsT_scale=act_scales[:, cols(first_pass + s, P)],
+                lhsT=act_codes[:, cols(act_pass(name, s), P)].bitcast(FP8X4),
+                lhsT_scale=act_scales[:, cols(act_pass(name, s), P)],
                 rhs=sq_codes[:, cols(place, WIDTH)].bitcast(FP8X4),
                 rhs_scale=sq_scales[:, cols(place, WIDTH)],
                 start=True,
@@ -279,22 +295,24 @@ def tile_relationalmemorycorecell_pa_k_kernel(
 
         for t in range(RAW_BUFS):
             load_pair(t)
-            load_chunk(t)
-        nc.sync.dma_start(out=mem[:], in_=m_state.rearrange("b s m -> b (s m)"))
+            if 1 <= t <= CHUNK_AHEAD:
+                load_chunk(t - 1)
 
         last_step = ready(2) + 2 + PICKUP + SLOTS - 1
         for t in range(-1, last_step + 1):
             if t >= 0:
                 for later in due(t + RAW_BUFS, 0, PAIRS):
                     load_pair(later)
-                for later in due(t + RAW_BUFS, 0, CHUNKS):
+                for later in due(t + CHUNK_AHEAD, 0, CHUNKS):
                     load_chunk(later)
+                if t == CHUNKS - CHUNK_AHEAD:
+                    nc.sync.dma_start(out=mem[:], in_=m_state.rearrange("b s m -> b (s m)"))
 
             for s in due(t, PROP_FIRST):
-                slot_product(ATT_PASS, s, 0)
+                slot_product("att", s, 0)
             for gate in range(3):
                 for s in due(t, ready(gate)):
-                    slot_product(H_PASS, s, gate + 1)
+                    slot_product("h", s, gate + 1)
             for c in due(t, CHUNK_FIRST, CHUNKS):
                 transpose_chunk(c)
             for later in due(t + 2, 0, PAIRS):
@@ -304,10 +322,11 @@ def tile_relationalmemorycorecell_pa_k_kernel(
             for gate in range(3):
                 for s in due(t, ready(gate) + 1):
                     gate_sum(gate, s)
-            for s in due(t, PROP_FIRST - 1):
-                nc.vector.tensor_tensor(out=prop[:, cols(s, WIDTH)], in0=b_g_rows[:], in1=att[:, cols(s, WIDTH)], op=ADD)
             for s in due(t, PROP_FIRST + 1):
                 nc.vector.tensor_tensor(out=prop[:, cols(s, WIDTH)], in0=products[(0, s)][:], in1=prop[:, cols(s, WIDTH)], op=ADD)
+            for s in due(t, PROP_FIRST - 1):
+                att = slot_rows[:, act_pass("att", s), :]
+                nc.vector.tensor_tensor(out=prop[:, cols(s, WIDTH)], in0=b_g_rows[:], in1=att, op=ADD)
             for s in due(t, ready(0) + 2 + PICKUP):
                 nc.vector.tensor_tensor(out=prop[:, cols(s, WIDTH)], in0=prop[:, cols(s, WIDTH)], in1=values[(0, s)][:], op=MULT)
             for s in due(t, ready(1) + 1 + PICKUP):
@@ -323,6 +342,8 @@ def tile_relationalmemorycorecell_pa_k_kernel(
                 nc.vector.tensor_tensor(out=result[:], in0=tanh_mem[:, cols(s, WIDTH)], in1=values[(2, s)][:], op=MULT)
                 nc.sync.dma_start(out=out_1[:, s, :], in_=result[:])
 
+            if t == 0:
+                quantise_pair(0)
             for later in due(t + 1, 0, PAIRS):
                 regroup_pair(later)
             for c in due(t, CHUNK_FIRST, CHUNKS):
@@ -332,8 +353,8 @@ def tile_relationalmemorycorecell_pa_k_kernel(
             for gate in range(3):
                 if t == ready(gate):
                     share(gate)
-            for now in due(t, 0, PAIRS):
-                quantise_pair(now)
+            for now in due(t, 1, PAIRS - 1):
+                quantise_pair(now + 1)
 
             for two in due(t, TANH_FIRST, SLOTS // 2):
                 nc.scalar.activation(out=tanh_mem[:, cols(two, 2 * WIDTH)], in_=mem[:, cols(two, 2 * WIDTH)], func=TANH)

@@ -213,11 +213,11 @@ def tile_relationalmemorycorecell_pa_k_kernel(
             elif t >= TENSOR_FIRST:
                 vector_boxes = [(0, slice(0, VECTOR_COLS))]
                 scalar_boxes = [(1, slice(VECTOR_COLS + TENSOR_COLS - WIDTH, WIDTH))]
-            for copy, parts in ((nc.vector.tensor_copy, vector_boxes), (nc.scalar.copy, scalar_boxes)):
+            for copy, parts, run in ((nc.vector.tensor_copy, vector_boxes, 4), (nc.scalar.copy, scalar_boxes, 8)):
                 for c, part in parts:
                     copy(
-                        out=grouped[:, c, part].rearrange("p (q i) j -> p q j i", i=4),
-                        in_=raw[:, c, :, part].rearrange("p j (q i) -> p q j i", i=4),
+                        out=grouped[:, c, part].rearrange("p (q i) j -> p q j i", i=run),
+                        in_=raw[:, c, :, part].rearrange("p j (q i) -> p q j i", i=run),
                     )
             if t >= TENSOR_FIRST:
                 flat = grouped[:].rearrange("p c n j -> p (c n) j")

@@ -34,7 +34,9 @@ RAW_BUFS = 5
 
 TENSOR_FIRST = 11
 TENSOR_COLS = 256
-VECTOR_COLS = 384
+VECTOR_COLS = 400
+
+GPSIMD_SLOTS = (0, 2, 4)
 
 PICKUP = 2
 CHUNK_FIRST = 0
@@ -57,6 +59,16 @@ def due(step, first, count=SLOTS):
 def act_pass(name, g):
     chunk, within = divmod(g, CHUNK_PASSES)
     return CHUNK_ORDER.index(name + "%d" % chunk) * CHUNK_PASSES + within
+
+
+def last_parts(s):
+    if s < SLOTS - 1:
+        return [cols(0, WIDTH)]
+    return [cols(half, WIDTH // 2) for half in range(2)]
+
+
+def sums_from(gate):
+    return ready(gate) + (1 if gate < 2 else 0)
 
 
 def ready(gate):
@@ -229,7 +241,7 @@ def tile_relationalmemorycorecell_pa_k_kernel(
             regroup_banks[t] = bank
             rest = VECTOR_COLS + TENSOR_COLS - WIDTH
             first = 0
-            for c, begin, end in ((0, VECTOR_COLS, WIDTH), (1, 0, rest)):
+            for c, begin, end in ((0, VECTOR_COLS, WIDTH), (1, 0, rest // 2), (1, rest // 2, rest)):
                 nc.tensor.matmul(
                     out=bank[:, first : first + end - begin, :],
                     lhsT=identity_b[:],
@@ -298,7 +310,7 @@ def tile_relationalmemorycorecell_pa_k_kernel(
             if 1 <= t <= CHUNK_AHEAD:
                 load_chunk(t - 1)
 
-        last_step = ready(2) + 2 + PICKUP + SLOTS - 1
+        last_step = sums_from(2) + 1 + PICKUP + SLOTS - 1
         for t in range(-1, last_step + 1):
             if t >= 0:
                 for later in due(t + RAW_BUFS, 0, PAIRS):
@@ -311,7 +323,7 @@ def tile_relationalmemorycorecell_pa_k_kernel(
             for s in due(t, PROP_FIRST):
                 slot_product("att", s, 0)
             for gate in range(3):
-                for s in due(t, ready(gate)):
+                for s in due(t, sums_from(gate) - 1):
                     slot_product("h", s, gate + 1)
             for c in due(t, CHUNK_FIRST, CHUNKS):
                 transpose_chunk(c)
@@ -319,8 +331,8 @@ def tile_relationalmemorycorecell_pa_k_kernel(
                 if later >= TENSOR_FIRST:
                     tensor_regroup(later)
 
-            for gate in range(3):
-                for s in due(t, ready(gate) + 1):
+            for gate in range(2):
+                for s in due(t, sums_from(gate)):
                     gate_sum(gate, s)
             for s in due(t, PROP_FIRST + 1):
                 nc.vector.tensor_tensor(out=prop[:, cols(s, WIDTH)], in0=products[(0, s)][:], in1=prop[:, cols(s, WIDTH)], op=ADD)
@@ -333,14 +345,20 @@ def tile_relationalmemorycorecell_pa_k_kernel(
                 result = work.tile([P, WIDTH], F32)
                 results[(1, s)] = result
                 nc.vector.tensor_tensor(out=result[:], in0=mem[:, cols(s, WIDTH)], in1=values[(1, s)][:], op=MULT)
+            if t == ready(2):
+                share(2)
+            for s in due(t, sums_from(2)):
+                gate_sum(2, s)
             for s in due(t, ready(1) + 1 + 2 * PICKUP):
                 result = results[(1, s)]
                 nc.vector.tensor_tensor(out=result[:], in0=result[:], in1=prop[:, cols(s, WIDTH)], op=ADD)
                 nc.sync.dma_start(out=out_0[:, s, :], in_=result[:])
-            for s in due(t, ready(2) + 2 + PICKUP):
+            for s in due(t, sums_from(2) + 1 + PICKUP):
                 result = work.tile([P, WIDTH], F32)
-                nc.vector.tensor_tensor(out=result[:], in0=tanh_mem[:, cols(s, WIDTH)], in1=values[(2, s)][:], op=MULT)
-                nc.sync.dma_start(out=out_1[:, s, :], in_=result[:])
+                engine = nc.gpsimd if s in GPSIMD_SLOTS else nc.vector
+                for part in last_parts(s):
+                    engine.tensor_tensor(out=result[:, part], in0=tanh_mem[:, cols(s, WIDTH)][:, part], in1=values[(2, s)][:, part], op=MULT)
+                    nc.sync.dma_start(out=out_1[:, s, part], in_=result[:, part])
 
             if t == 0:
                 quantise_pair(0)
@@ -350,7 +368,7 @@ def tile_relationalmemorycorecell_pa_k_kernel(
                 collect_chunk(c)
             for c in due(t, CHUNK_FIRST + 1, CHUNKS):
                 quantise_chunk(c)
-            for gate in range(3):
+            for gate in range(2):
                 if t == ready(gate):
                     share(gate)
             for now in due(t, 1, PAIRS - 1):
@@ -359,10 +377,11 @@ def tile_relationalmemorycorecell_pa_k_kernel(
             for two in due(t, TANH_FIRST, SLOTS // 2):
                 nc.scalar.activation(out=tanh_mem[:, cols(two, 2 * WIDTH)], in_=mem[:, cols(two, 2 * WIDTH)], func=TANH)
             for gate in (0, 2):
-                for s in due(t, ready(gate) + 1):
+                for s in due(t, sums_from(gate)):
                     sigmoid(values[(gate, s)][:])
-                for s in due(t, ready(gate) + 2):
-                    sigmoid(values[(gate, s)][:])
+                for s in due(t, sums_from(gate) + 1):
+                    for part in last_parts(s) if gate == 2 else [cols(0, WIDTH)]:
+                        sigmoid(values[(gate, s)][:, part])
             for s in due(t, ready(1) + 1):
                 sigmoid(values[(1, s)][:])
             for s in due(t, ready(1) + 1 + PICKUP):

from contextlib import ExitStack

import concourse.mybir as mybir
from concourse.masks import make_identity

F32 = mybir.dt.float32
BF16 = mybir.dt.bfloat16
U32 = mybir.dt.uint32
U8 = mybir.dt.uint8
I32 = mybir.dt.int32
FP8X4 = mybir.dt.float8_e4m3fn_x4
ADD = mybir.AluOpType.add
MULT = mybir.AluOpType.mult
SIGMOID = mybir.ActivationFunctionType.Sigmoid
TANH = mybir.ActivationFunctionType.Tanh

P = 128
PACK = 4
K_PASS = P * PACK
SLOTS = 8
WIDTH = 512
D_IN = 8192
FORGET_BIAS = 1.0

CHUNK_PASSES = 4
CHUNK = CHUNK_PASSES * K_PASS
CHUNK_ORDER = ("att0", "x0", "x1", "att1", "x2", "x3", "h0", "h1")
CHUNKS = len(CHUNK_ORDER)

SQUARE_PAIRS = 2
GATE_PAIRS = D_IN // (2 * K_PASS)
PAIRS = SQUARE_PAIRS + 3 * GATE_PAIRS
RAW_BUFS = 5

TENSOR_FIRST = 11
TENSOR_COLS = 256
VECTOR_COLS = 400

GPSIMD_SLOTS = (0, 2, 4)

PICKUP = 2
CHUNK_FIRST = 0
CHUNK_AHEAD = 4
PROP_FIRST = CHUNK_FIRST + 2
TANH_FIRST = CHUNK_FIRST + CHUNKS

FLOPS = 2 * P * D_IN * WIDTH * 3 + 2 * P * SLOTS * WIDTH * WIDTH * 4


def cols(index, width):
    return slice(index * width, (index + 1) * width)


def due(step, first, count=SLOTS):
    item = step - first
    return [item] if 0 <= item < count else []


def act_pass(name, g):
    chunk, within = divmod(g, CHUNK_PASSES)
    return CHUNK_ORDER.index(name + "%d" % chunk) * CHUNK_PASSES + within


def last_parts(s):
    if s < SLOTS - 1:
        return [cols(0, WIDTH)]
    return [cols(half, WIDTH // 2) for half in range(2)]


def sums_from(gate):
    return ready(gate) + (1 if gate < 2 else 0)


def ready(gate):
    return SQUARE_PAIRS + GATE_PAIRS * (gate + 1)


def tile_relationalmemorycorecell_pa_k_kernel(
    tc,
    inputs,
    h_state,
    m_state,
    mem_att,
    W_g,
    b_g,
    W_wf,
    W_wi,
    W_wo,
    W_uf,
    b_uf,
    W_ui,
    b_ui,
    W_uo,
    b_uo,
    out_0,
    out_1,
):
    nc = tc.nc
    input_weights = (W_wi, W_wf, W_wo)
    square_weights = (W_g, W_ui, W_uf, W_uo)
    gate_biases = (b_ui, b_uf, b_uo)

    with ExitStack() as ctx:
        keep = ctx.enter_context(tc.tile_pool(name="keep", bufs=1))
        turned_pool = ctx.enter_context(tc.tile_pool(name="turned", bufs=2))
        raw_pool = ctx.enter_context(tc.tile_pool(name="raw", bufs=RAW_BUFS))
        stream = ctx.enter_context(tc.tile_pool(name="stream", bufs=3))
        work = ctx.enter_context(tc.tile_pool(name="work", bufs=5))
        turn_psum = ctx.enter_context(tc.psum_pool(name="turn_psum", bufs=2))
        x_psum = ctx.enter_context(tc.psum_pool(name="x_psum", bufs=1))
        bias_psum = ctx.enter_context(tc.psum_pool(name="bias_psum", bufs=1))
        slot_psum = ctx.enter_context(tc.psum_pool(name="slot_psum", bufs=4))
        ctx.enter_context(tc.manual_schedule())

        b_g_row = keep.tile([P, WIDTH], BF16)
        nc.vector.memset(b_g_row[:].bitcast(I32), 0)
        ones = keep.tile([P, P], BF16)
        nc.gpsimd.memset(ones[:], 1.0)
        identity = keep.tile([P, P], F32)
        make_identity(nc, identity[:])
        identity_b = keep.tile([P, P], BF16)
        make_identity(nc, identity_b[:])
        nc.scalar.dma_start(out=b_g_row[0:1, :], in_=b_g.unsqueeze(0))
        b_g_rows = bias_psum.tile([P, WIDTH], F32)
        nc.tensor.matmul(out=b_g_rows[:], lhsT=ones[:], rhs=b_g_row[:], start=True, stop=True)

        warm = keep.tile([P, 1], F32)
        nc.scalar.activation(out=warm[:], in_=ones[:, 0:1], func=SIGMOID)

        rows = keep.tile([P, CHUNKS, CHUNK], BF16)
        slot_rows = rows[:].rearrange("b c (g k) -> b (c g) k", g=CHUNK_PASSES)
        mem = keep.tile([P, SLOTS * WIDTH], BF16)
        act_codes = keep.tile([P, CHUNKS * CHUNK_PASSES * P], U32, align_bytes=64)
        act_scales = keep.tile([P, CHUNKS * CHUNK_PASSES * P], U8, align_bytes=64)
        sq_codes = keep.tile([P, 4 * WIDTH], U32, align_bytes=64)
        sq_scales = keep.tile([P, 4 * WIDTH], U8, align_bytes=64)
        bias_rows = keep.tile([P, 3, WIDTH], BF16)
        prop = keep.tile([P, SLOTS * WIDTH], F32)
        tanh_mem = keep.tile([P, SLOTS * WIDTH], F32)

        raw_tiles = {}
        regroup_banks = {}
        grouped_tiles = {}
        bank_tiles = {}
        turned_tiles = {}
        totals = {}
        shared = {}
        products = {}
        values = {}
        results = {}

        def load_chunk(c):
            sources = {
                "x": inputs,
                "h": h_state.rearrange("b s m -> b (s m)"),
                "att": mem_att.rearrange("b s m -> b (s m)"),
            }
            name = CHUNK_ORDER[c]
            source = sources[name[:-1]][:, cols(int(name[-1]), CHUNK)]
            nc.sync.dma_start(out=rows[:, c, :], in_=source)

        def load_bias(gate):
            nc.sync.dma_start(out=bias_rows[:, gate, :], in_=gate_biases[gate].partition_broadcast(P))

        def load_pair(t):
            raw = raw_pool.tile([P, 2, PACK, WIDTH], BF16)
            raw_tiles[t] = raw
            if t == 0:
                for piece in range(2):
                    for c in range(2):
                        nc.sync.dma_start(
                            out=raw[:, c, :, cols(piece, WIDTH // 2)],
                            in_=square_weights[c].rearrange("(p j) n -> p j n", j=PACK)[:, :, cols(piece, WIDTH // 2)],
                        )
                return
            if t < SQUARE_PAIRS:
                for c in range(2):
                    nc.sync.dma_start(out=raw[:, c], in_=square_weights[2 * t + c].rearrange("(p j) n -> p j n", j=PACK))
                return
            gate, pair = divmod(t - SQUARE_PAIRS, GATE_PAIRS)
            nc.sync.dma_start(
                out=raw[:],
                in_=input_weights[gate][cols(pair, 2 * K_PASS), :].rearrange("(c p j) n -> p c j n", p=P, j=PACK),
            )
            if pair == GATE_PAIRS - 1:
                load_bias(gate)

        def transpose_chunk(c):
            words = rows[:, c, :].bitcast(F32).rearrange("b (g p u) -> b g p u", p=P, u=2)
            for half in range(CHUNK_PASSES // 2):
                bank = turn_psum.tile([P, 2, 2, P], F32)
                bank_tiles[(c, half)] = bank
                for g in range(2):
                    for u in range(2):
                        nc.tensor.transpose(bank[:, g, u, :], words[:, 2 * half + g, :, u], identity[:])

        def collect_chunk(c):
            turned = turned_pool.tile([P, CHUNK_PASSES * P * PACK], BF16, align_bytes=64)
            turned_tiles[c] = turned
            turned_words = turned[:].bitcast(F32).rearrange("p (g b u) -> p g b u", b=P, u=2)
            for half in range(CHUNK_PASSES // 2):
                nc.scalar.copy(
                    out=turned_words[:, cols(half, 2)],
                    in_=bank_tiles[(c, half)][:].rearrange("p g u b -> p g b u"),
                )

        def quantise_chunk(c):
            nc.vector.quantize_mx(
                out=act_codes[:, cols(c, CHUNK_PASSES * P)].bitcast(FP8X4),
                scales=act_scales[:, cols(c, CHUNK_PASSES * P)],
                in_=turned_tiles[c][:],
            )

        def regroup_pair(t):
            raw = raw_tiles[t]
            grouped = stream.tile([P, 2, WIDTH, PACK], BF16, align_bytes=64)
            grouped_tiles[t] = grouped
            vector_boxes, scalar_boxes = [(0, cols(0, WIDTH))], [(1, cols(0, WIDTH))]
            if t == 0:
                vector_boxes = [(0, cols(0, WIDTH // 2)), (0, cols(1, WIDTH // 2)), (1, cols(1, WIDTH // 2))]
                scalar_boxes = [(1, cols(0, WIDTH // 2))]
            elif t == 1:
                vector_boxes = [(0, cols(0, WIDTH)), (1, cols(0, WIDTH // 2))]
                scalar_boxes = [(1, cols(1, WIDTH // 2))]
            elif t >= TENSOR_FIRST:
                vector_boxes = [(0, slice(0, VECTOR_COLS))]
                scalar_boxes = [(1, slice(VECTOR_COLS + TENSOR_COLS - WIDTH, WIDTH))]
            for copy, parts, run in ((nc.vector.tensor_copy, vector_boxes, 4), (nc.scalar.copy, scalar_boxes, 8)):
                for c, part in parts:
                    copy(
                        out=grouped[:, c, part].rearrange("p (q i) j -> p q j i", i=run),
                        in_=raw[:, c, :, part].rearrange("p j (q i) -> p q j i", i=run),
                    )
            if t >= TENSOR_FIRST:
                flat = grouped[:].rearrange("p c n j -> p (c n) j")
                nc.scalar.copy(out=flat[:, VECTOR_COLS : VECTOR_COLS + TENSOR_COLS, :], in_=regroup_banks[t][:])

        def tensor_regroup(t):
            raw = raw_tiles[t]
            bank = turn_psum.tile([P, TENSOR_COLS, PACK], BF16)
            regroup_banks[t] = bank
            rest = VECTOR_COLS + TENSOR_COLS - WIDTH
            first = 0
            for c, begin, end in ((0, VECTOR_COLS, WIDTH), (1, 0, rest // 2), (1, rest // 2, rest)):
                nc.tensor.matmul(
                    out=bank[:, first : first + end - begin, :],
                    lhsT=identity_b[:],
                    rhs=raw[:, c, :, begin:end].rearrange("p j n -> p n j"),
                    start=True,
                    stop=True,
                )
                first += end - begin

        def quantise_pair(t):
            grouped = grouped_tiles[t][:].rearrange("p c n j -> p (c n j)")
            if t < SQUARE_PAIRS:
                nc.vector.quantize_mx(
                    out=sq_codes[:, cols(t, 2 * WIDTH)].bitcast(FP8X4),
                    scales=sq_scales[:, cols(t, 2 * WIDTH)],
                    in_=grouped,
                )
                return
            codes = stream.tile([P, 2 * WIDTH], U32, align_bytes=64)
            scales = stream.tile([P, 2 * WIDTH], U8, align_bytes=64)
            nc.vector.quantize_mx(out=codes[:].bitcast(FP8X4), scales=scales[:], in_=grouped)
            gate, pair = divmod(t - SQUARE_PAIRS, GATE_PAIRS)
            if pair == 0:
                total = x_psum.tile([P, WIDTH], F32)
                totals[gate] = total
            for c in range(2):
                g = 2 * pair + c
                nc.tensor.matmul_mx(
                    out=totals[gate][:],
                    lhsT=act_codes[:, cols(act_pass("x", g), P)].bitcast(FP8X4),
                    lhsT_scale=act_scales[:, cols(act_pass("x", g), P)],
                    rhs=codes[:, cols(c, WIDTH)].bitcast(FP8X4),
                    rhs_scale=scales[:, cols(c, WIDTH)],
                    start=(g == 0),
                    stop=(g == 2 * GATE_PAIRS - 1),
                )

        def share(gate):
            common = keep.tile([P, WIDTH], F32, name="common%d" % gate)
            shared[gate] = common
            nc.vector.tensor_tensor(out=common[:], in0=totals[gate][:], in1=bias_rows[:, gate, :], op=ADD)

        def slot_product(name, s, place):
            product = slot_psum.tile([P, WIDTH], F32)
            products[(place, s)] = product
            nc.tensor.matmul_mx(
                out=product[:],
                lhsT=act_codes[:, cols(act_pass(name, s), P)].bitcast(FP8X4),
                lhsT_scale=act_scales[:, cols(act_pass(name, s), P)],
                rhs=sq_codes[:, cols(place, WIDTH)].bitcast(FP8X4),
                rhs_scale=sq_scales[:, cols(place, WIDTH)],
                start=True,
                stop=True,
            )

        def gate_sum(gate, s):
            value = work.tile([P, WIDTH], F32)
            values[(gate, s)] = value
            nc.vector.tensor_tensor(out=value[:], in0=products[(gate + 1, s)][:], in1=shared[gate][:], op=ADD)

        def sigmoid(tile_ap, bias=0.0):
            nc.scalar.activation(out=tile_ap, in_=tile_ap, func=SIGMOID, bias=bias)

        for t in range(RAW_BUFS):
            load_pair(t)
            if 1 <= t <= CHUNK_AHEAD:
                load_chunk(t - 1)

        last_step = sums_from(2) + 1 + PICKUP + SLOTS - 1
        for t in range(-1, last_step + 1):
            if t >= 0:
                for later in due(t + RAW_BUFS, 0, PAIRS):
                    load_pair(later)
                for later in due(t + CHUNK_AHEAD, 0, CHUNKS):
                    load_chunk(later)
                if t == CHUNKS - CHUNK_AHEAD:
                    nc.sync.dma_start(out=mem[:], in_=m_state.rearrange("b s m -> b (s m)"))

            for s in due(t, PROP_FIRST):
                slot_product("att", s, 0)
            for gate in range(3):
                for s in due(t, sums_from(gate) - 1):
                    slot_product("h", s, gate + 1)
            for c in due(t, CHUNK_FIRST, CHUNKS):
                transpose_chunk(c)
            for later in due(t + 2, 0, PAIRS):
                if later >= TENSOR_FIRST:
                    tensor_regroup(later)

            for gate in range(2):
                for s in due(t, sums_from(gate)):
                    gate_sum(gate, s)
            for s in due(t, PROP_FIRST + 1):
                nc.vector.tensor_tensor(out=prop[:, cols(s, WIDTH)], in0=products[(0, s)][:], in1=prop[:, cols(s, WIDTH)], op=ADD)
            for s in due(t, PROP_FIRST - 1):
                att = slot_rows[:, act_pass("att", s), :]
                nc.vector.tensor_tensor(out=prop[:, cols(s, WIDTH)], in0=b_g_rows[:], in1=att, op=ADD)
            for s in due(t, ready(0) + 2 + PICKUP):
                nc.vector.tensor_tensor(out=prop[:, cols(s, WIDTH)], in0=prop[:, cols(s, WIDTH)], in1=values[(0, s)][:], op=MULT)
            for s in due(t, ready(1) + 1 + PICKUP):
                result = work.tile([P, WIDTH], F32)
                results[(1, s)] = result
                nc.vector.tensor_tensor(out=result[:], in0=mem[:, cols(s, WIDTH)], in1=values[(1, s)][:], op=MULT)
            if t == ready(2):
                share(2)
            for s in due(t, sums_from(2)):
                gate_sum(2, s)
            for s in due(t, ready(1) + 1 + 2 * PICKUP):
                result = results[(1, s)]
                nc.vector.tensor_tensor(out=result[:], in0=result[:], in1=prop[:, cols(s, WIDTH)], op=ADD)
                nc.sync.dma_start(out=out_0[:, s, :], in_=result[:])
            for s in due(t, sums_from(2) + 1 + PICKUP):
                result = work.tile([P, WIDTH], F32)
                engine = nc.gpsimd if s in GPSIMD_SLOTS else nc.vector
                for part in last_parts(s):
                    engine.tensor_tensor(out=result[:, part], in0=tanh_mem[:, cols(s, WIDTH)][:, part], in1=values[(2, s)][:, part], op=MULT)
                    nc.sync.dma_start(out=out_1[:, s, part], in_=result[:, part])

            if t == 0:
                quantise_pair(0)
            for later in due(t + 1, 0, PAIRS):
                regroup_pair(later)
            for c in due(t, CHUNK_FIRST, CHUNKS):
                collect_chunk(c)
            for c in due(t, CHUNK_FIRST + 1, CHUNKS):
                quantise_chunk(c)
            for gate in range(2):
                if t == ready(gate):
                    share(gate)
            for now in due(t, 1, PAIRS - 1):
                quantise_pair(now + 1)

            for two in due(t, TANH_FIRST, SLOTS // 2):
                nc.scalar.activation(out=tanh_mem[:, cols(two, 2 * WIDTH)], in_=mem[:, cols(two, 2 * WIDTH)], func=TANH)
            for gate in (0, 2):
                for s in due(t, sums_from(gate)):
                    sigmoid(values[(gate, s)][:])
                for s in due(t, sums_from(gate) + 1):
                    for part in last_parts(s) if gate == 2 else [cols(0, WIDTH)]:
                        sigmoid(values[(gate, s)][:, part])
            for s in due(t, ready(1) + 1):
                sigmoid(values[(1, s)][:])
            for s in due(t, ready(1) + 1 + PICKUP):
                sigmoid(results[(1, s)][:], bias=FORGET_BIAS)
